import numpy as np
import ml_dtypes


def mxq(x, axis, fmt="e4m3"):
    dtype, down = {"e4m3": (ml_dtypes.float8_e4m3fn, 7), "e5m2": (ml_dtypes.float8_e5m2, 14)}[fmt]
    v = np.moveaxis(np.asarray(x, np.float32).astype(ml_dtypes.bfloat16).astype(np.float64), axis, -1)
    blocks = v.reshape(v.shape[:-1] + (-1, 32))
    amax = np.abs(blocks).max(-1, keepdims=True)
    byte = np.maximum(np.where(amax > 0, np.frexp(amax)[1] - 1 + 127, 0) - down, 1)
    scale = np.exp2(byte - 127.0)
    codes = (blocks / scale).astype(np.float32).astype(dtype).astype(np.float64)
    return np.moveaxis((codes * scale).reshape(v.shape), -1, axis)


WIDE = False


def mx_kscale(k):
    if not WIDE:
        return np.ones(k)
    levels = np.array([10, -10, 5, -5, 0])
    if k % 512:
        return np.exp2(np.random.permutation(np.resize(levels, k // 32))).repeat(32)
    a = np.empty((k // 512, 16))
    for p in range(k // 512):
        a[p, :8] = np.random.permutation(np.resize(levels, 8))
        for g in range(8):
            far = levels[np.abs(levels - a[p, g]) >= 10]
            a[p, g + 8] = far[np.random.randint(len(far))]
    return np.exp2(a.ravel()).repeat(32)


BF16 = ml_dtypes.bfloat16


def bf(x):
    return np.asarray(x, np.float32).astype(BF16)


def f64(x):
    return np.asarray(x).astype(np.float64)


B, H, W, C, HIDDEN = 4, 16, 16, 512, 2048


def _perceive(x):
    r = lambda di, dj: np.roll(x, shift=(-di, -dj), axis=(1, 2))
    sx = (r(-1, 1) - r(-1, -1)) + 2.0 * (r(0, 1) - r(0, -1)) + (r(1, 1) - r(1, -1))
    sy = (r(1, -1) - r(-1, -1)) + 2.0 * (r(1, 0) - r(-1, 0)) + (r(1, 1) - r(-1, 1))
    return np.concatenate([sx, sy, x], axis=-1)


def draw0():
    s = mx_kscale(C)
    s3 = np.tile(s, 3)
    t = mx_kscale(HIDDEN)
    return {"state_grid": bf(np.random.standard_normal((B, H, W, C)) * s),
            "W_hidden": bf(np.random.standard_normal((HIDDEN, 3 * C)) * 0.6 / np.sqrt(3 * C) / s3[None, :] * t[:, None]),
            "W_out": bf(np.random.standard_normal((C, HIDDEN)) / np.sqrt(HIDDEN) / t[None, :])}


def core(state_grid, W_hidden, W_out):
    perception = _perceive(f64(state_grid))
    hidden = np.maximum(mxq(perception, 3, "e4m3") @ mxq(f64(W_hidden), 1, "e4m3").T, 0.0)
    delta_s = mxq(hidden, 3, "e4m3") @ mxq(f64(W_out), 1, "e4m3").T
    return delta_s


def e4m3fn_bytes(y):
    return np.clip(np.asarray(y, np.float64), -448.0, 448.0).astype(np.float32).astype(ml_dtypes.float8_e4m3fn).view(np.uint8)


def e4m3fn_values(b):
    return np.asarray(b, np.uint8).view(ml_dtypes.float8_e4m3fn).astype(np.float64)


def setup_inputs():
    d = draw0()
    x0 = np.asarray(d['W_out']).astype(np.float64)
    s = (np.max(np.abs(x0), axis=(0,), keepdims=True) / 448.0).astype(np.float32)
    out = {}
    for k, v in d.items():
        if k == 'W_out':
            out['W_out_bytes'] = e4m3fn_bytes(x0 / s.astype(np.float64))
            out['W_out_scale'] = s
        else:
            out[k] = v
    return out


def reference(state_grid, W_hidden, W_out_bytes, W_out_scale):
    return core(state_grid, W_hidden, e4m3fn_values(W_out_bytes) * W_out_scale.astype(np.float64))

@@ -1,0 +1,320 @@
+from contextlib import ExitStack
+
+import concourse.mybir as mybir
+from concourse.masks import make_identity
+
+F32 = mybir.dt.float32
+BF16 = mybir.dt.bfloat16
+U32 = mybir.dt.uint32
+U8 = mybir.dt.uint8
+FP8 = mybir.dt.float8_e4m3fn
+FP8X4 = mybir.dt.float8_e4m3fn_x4
+ALU = mybir.AluOpType
+ACT = mybir.ActivationFunctionType
+
+P = 128
+BATCH, HEIGHT, WIDTH, CH, HIDDEN = 4, 16, 16, 512, 2048
+GRID = HEIGHT * WIDTH
+TOKENS = BATCH * GRID
+PASSES1 = 3 * CH // 512
+GROUPS = HIDDEN // 512
+CHUNKS = TOKENS // P
+FLOPS = 2 * TOKENS * 3 * CH * HIDDEN + 2 * TOKENS * HIDDEN * CH
+
+
+def tile_nn_kernel(tc, state_grid, W_hidden, W_out_bytes, W_out_scale, out):
+    nc = tc.nc
+    x_hbm = state_grid.rearrange("b i j c -> (b i j) c")
+    out_hbm = out.rearrange("b i j c -> (b i j) c")
+
+    with ExitStack() as ctx:
+        keep = ctx.enter_context(tc.tile_pool(name="keep", bufs=1))
+        work = ctx.enter_context(tc.tile_pool(name="work", bufs=3))
+        psum = ctx.enter_context(tc.psum_pool(name="psum", bufs=8))
+        ctx.enter_context(tc.manual_schedule())
+
+        def new_bank():
+            bank = psum.tile([P, 512], F32, name="bank")
+            return bank
+
+        x_nat = keep.tile([P, 2 * BATCH, CH], BF16, name="x_nat")
+        x_shift = keep.tile([P, 2 * BATCH, CH], BF16, name="x_shift")
+        w_raw = keep.tile([P, GROUPS, 4, 3 * CH], BF16, name="w_raw")
+        wo_bytes = keep.tile([P, 4, HIDDEN], U8, name="wo_bytes")
+        wo_scale = keep.tile([P, HIDDEN], F32, name="wo_scale")
+        w_hbm = W_hidden.rearrange("(g m t) k -> g m t k", m=P, t=4)
+
+        def load_x(b):
+            t0 = b * GRID
+            nc.sync.dma_start(
+                out=x_nat[:, 2 * b : 2 * b + 2, :],
+                in_=x_hbm[t0 : t0 + GRID, :].rearrange("(s p) c -> p s c", p=P),
+            )
+            nc.sync.dma_start(out=x_shift[:, 2 * b, :], in_=x_hbm[t0 + 64 : t0 + 192, :])
+            nc.sync.dma_start(out=x_shift[0:64, 2 * b + 1, :], in_=x_hbm[t0 + 192 : t0 + 256, :])
+            nc.sync.dma_start(out=x_shift[64:128, 2 * b + 1, :], in_=x_hbm[t0 : t0 + 64, :])
+
+        def load_w_pass(g, k):
+            nc.sync.dma_start(
+                out=w_raw[:, g, :, k * 512 : (k + 1) * 512],
+                in_=w_hbm[g][:, :, k * 512 : (k + 1) * 512],
+            )
+
+        load_x(0)
+        load_w_pass(0, 0)
+        load_w_pass(0, 1)
+        load_w_pass(0, 2)
+        load_x(1)
+        load_x(2)
+        load_x(3)
+        nc.sync.dma_start(out=w_raw[:, 1], in_=w_hbm[1])
+        nc.sync.dma_start(out=wo_bytes[:], in_=W_out_bytes.rearrange("(r p) k -> p r k", p=P))
+        nc.sync.dma_start(
+            out=wo_scale[:], in_=W_out_scale.rearrange("o k -> (o k)").partition_broadcast(P)
+        )
+        nc.sync.dma_start(out=w_raw[:, 2], in_=w_hbm[2])
+        nc.sync.dma_start(out=w_raw[:, 3], in_=w_hbm[3])
+
+        warm = keep.tile([P, 1], F32, name="warm")
+        nc.vector.memset(warm[:], 0.0)
+        nc.scalar.activation(out=warm[:], in_=warm[:], func=ACT.Relu)
+
+        ident_b = keep.tile([P, P], BF16, name="ident_b")
+        ident_f = keep.tile([P, P], F32, name="ident_f")
+        make_identity(nc, ident_b[:])
+        nc.vector.tensor_copy(out=ident_f[:], in_=ident_b[:])
+        padded = keep.tile([P, 8, 18], BF16, name="padded")
+        ident_rows = ident_b[:].rearrange("p (i j) -> p i j", j=16)
+        nc.vector.tensor_copy(out=padded[:, :, 1:17], in_=ident_rows)
+        nc.vector.tensor_copy(out=padded[:, :, 0:1], in_=ident_rows[:, :, 15:16])
+        nc.vector.tensor_copy(out=padded[:, :, 17:18], in_=ident_rows[:, :, 0:1])
+        diff = keep.tile([P, P], BF16, name="diff")
+        smooth = keep.tile([P, P], BF16, name="smooth")
+        part = keep.tile([P, P], BF16, name="part")
+        sobel = keep.tile([P, 2, 64], BF16, name="sobel")
+        rows16 = "p (i j) -> p i j"
+        nc.vector.tensor_tensor(
+            out=diff[:].rearrange(rows16, j=16), in0=padded[:, :, 2:18], in1=padded[:, :, 0:16], op=ALU.subtract
+        )
+        nc.vector.tensor_tensor(
+            out=part[:].rearrange(rows16, j=16), in0=padded[:, :, 2:18], in1=padded[:, :, 0:16], op=ALU.add
+        )
+        nc.vector.scalar_tensor_tensor(
+            out=smooth[:], in0=ident_b[:], scalar=2.0, in1=part[:], op0=ALU.mult, op1=ALU.add
+        )
+        around = keep.tile([P, 64], BF16, name="around")
+        nc.vector.tensor_tensor(out=around[:], in0=diff[:, 16:80], in1=diff[:, 48:112], op=ALU.add)
+        nc.vector.scalar_tensor_tensor(
+            out=sobel[:, 0, :], in0=diff[:, 32:96], scalar=2.0, in1=around[:], op0=ALU.mult, op1=ALU.add
+        )
+        nc.vector.tensor_tensor(out=sobel[:, 1, :], in0=smooth[:, 48:112], in1=smooth[:, 16:80], op=ALU.subtract)
+        sobel_cols = sobel[:].rearrange("p f n -> p (f n)")
+
+        x_codes = keep.tile([P, BATCH, 3, GRID], U32, name="x_codes", align_bytes=64)
+        x_scales = keep.tile([P, BATCH, 3, GRID], U8, name="x_scales", align_bytes=64)
+        w_codes = keep.tile([P, GROUPS, 3, 512], U32, name="w_codes", align_bytes=64)
+        w_scales = keep.tile([P, GROUPS, 3, 512], U8, name="w_scales", align_bytes=64)
+        h_codes = keep.tile([P, GROUPS, TOKENS], U32, name="h_codes", align_bytes=64)
+        h_scales = keep.tile([P, GROUPS, TOKENS], U8, name="h_scales", align_bytes=64)
+        wo_codes = keep.tile([P, GROUPS, CH], U32, name="wo_codes", align_bytes=64)
+        wo_scales = keep.tile([P, GROUPS, CH], U8, name="wo_scales", align_bytes=64)
+        wo_bf = keep.tile([P, 4, HIDDEN], BF16, name="wo_bf")
+
+        def copy_out(engine, out_ap, in_ap):
+            if engine == "S":
+                nc.scalar.copy(out=out_ap, in_=in_ap)
+            else:
+                nc.vector.tensor_copy(out=out_ap, in_=in_ap)
+
+        pending = []
+
+        def flush():
+            while pending:
+                pending.pop(0)()
+
+        def sobel_step(b):
+            g12 = work.tile([P, 2, GRID, 4], BF16, name="g12", align_bytes=64)
+            g3 = work.tile([P, GRID, 4], BF16, name="g3", align_bytes=64)
+            tiles = [
+                (x_nat, 2 * b, 32, "S"),
+                (x_shift, 2 * b, 96, "V"),
+                (x_nat, 2 * b + 1, 160, "S"),
+                (x_shift, 2 * b + 1, None, "V"),
+            ]
+            banks = []
+            for src, slot, first, eng in tiles:
+                bank = new_bank()
+                banks.append(bank)
+                for t in range(4):
+                    nc.tensor.matmul(
+                        bank[:, t * P : (t + 1) * P], src[:, slot, t::4], sobel_cols, start=True, stop=True
+                    )
+            xbank = new_bank()
+            for s in range(2):
+                words = x_nat[:, 2 * b + s, :].bitcast(F32)
+                for u in range(2):
+                    q = 2 * s + u
+                    nc.tensor.transpose(xbank[:, q * P : (q + 1) * P], words[:, u::2], ident_f[:])
+            flush()
+            for (src, slot, first, eng), bank in zip(tiles, banks):
+                view = bank[:].rearrange("p (t f n) -> p f n t", t=4, f=2)
+                if first is None:
+                    copy_out(eng, g12[:, :, 224:256, :], view[:, :, 0:32, :])
+                    copy_out(eng, g12[:, :, 0:32, :], view[:, :, 32:64, :])
+                else:
+                    copy_out(eng, g12[:, :, first : first + 64, :], view)
+            copy_out(
+                "S",
+                g3[:].bitcast(F32).rearrange("p (s r) u -> p s r u", s=2),
+                xbank[:].rearrange("p (s u r) -> p s r u", s=2, u=2),
+            )
+
+            def quant():
+                nc.vector.quantize_mx(
+                    out=x_codes[:, b, 0:2, :].rearrange("p f n -> p (f n)").bitcast(FP8X4),
+                    scales=x_scales[:, b, 0:2, :].rearrange("p f n -> p (f n)"),
+                    in_=g12[:].rearrange("p f n t -> p (f n t)"),
+                )
+                nc.vector.quantize_mx(
+                    out=x_codes[:, b, 2, :].bitcast(FP8X4),
+                    scales=x_scales[:, b, 2, :],
+                    in_=g3[:].rearrange("p n t -> p (n t)"),
+                )
+
+            pending.append(quant)
+
+        def turn_step(sources, codes, scales, engines):
+            grouped = work.tile([P, 4, P, 4], BF16, name="grouped", align_bytes=64)
+            banks = []
+            for h in range(2):
+                bank = new_bank()
+                banks.append(bank)
+                for c in range(2):
+                    for u in range(2):
+                        q = 2 * c + u
+                        nc.tensor.transpose(
+                            bank[:, q * P : (q + 1) * P], sources[2 * h + c][:, u::2], ident_f[:]
+                        )
+            flush()
+            for h in range(2):
+                copy_out(
+                    engines[h],
+                    grouped[:, 2 * h : 2 * h + 2].bitcast(F32),
+                    banks[h][:].rearrange("p (c u r) -> p c r u", c=2, u=2),
+                )
+
+            def quant():
+                nc.vector.quantize_mx(
+                    out=codes.bitcast(FP8X4), scales=scales, in_=grouped[:].rearrange("p c r t -> p (c r t)")
+                )
+
+            pending.append(quant)
+
+        def w_step(g, k, engines):
+            sources = [w_raw[:, g, t, k * 512 : (k + 1) * 512].bitcast(F32) for t in range(4)]
+            turn_step(sources, w_codes[:, g, k, :], w_scales[:, g, k, :], engines)
+
+        def wo_step(g, engines):
+            sources = [wo_bf[:, r, g * 512 : (g + 1) * 512].bitcast(F32) for r in range(4)]
+            turn_step(sources, wo_codes[:, g, :], wo_scales[:, g, :], engines)
+
+        def wo_product(g, r):
+            cols = slice(g * 512, (g + 1) * 512)
+            nc.vector.tensor_tensor(
+                out=wo_bf[:, r, cols], in0=wo_bytes[:, r, cols].bitcast(FP8), in1=wo_scale[:, cols], op=ALU.mult
+            )
+
+        hid_tiles = {}
+
+        def s1_step(g, c, engine, width):
+            b, half = c // 2, c % 2
+            toks = slice(half * P, half * P + P)
+            bank = new_bank()
+            for t in range(4):
+                for k in range(3):
+                    nc.tensor.matmul_mx(
+                        out=bank[:, t * P : (t + 1) * P],
+                        lhsT=w_codes[:, g, k, t * P : (t + 1) * P].bitcast(FP8X4),
+                        lhsT_scale=w_scales[:, g, k, t * P : (t + 1) * P],
+                        rhs=x_codes[:, b, k, toks].bitcast(FP8X4),
+                        rhs_scale=x_scales[:, b, k, toks],
+                        start=(k == 0),
+                        stop=(k == 2),
+                    )
+            flush()
+            j = c % width
+            if j == 0:
+                hid = work.tile([P, 2 * P, 4], BF16, name="hid", align_bytes=64)
+                hid_tiles[0] = hid
+            hid = hid_tiles[0]
+            view = bank[:].rearrange("p (t n) -> p n t", t=4)
+            dst = hid[:, j * P : (j + 1) * P, :]
+            if engine == "S":
+                nc.scalar.activation(out=dst, in_=view, func=ACT.Relu)
+            else:
+                nc.vector.tensor_scalar_max(dst, view, 0.0)
+            if j == width - 1:
+                cols = slice((c + 1 - width) * P, (c + 1) * P)
+
+                def quant():
+                    nc.vector.quantize_mx(
+                        out=h_codes[:, g, cols].bitcast(FP8X4),
+                        scales=h_scales[:, g, cols],
+                        in_=hid[:, 0 : width * P, :].rearrange("p n t -> p (n t)"),
+                    )
+
+                pending.append(quant)
+
+        def s2_step(c, engine):
+            toks = slice(c * P, (c + 1) * P)
+            bank = new_bank()
+            for g in range(GROUPS):
+                nc.tensor.matmul_mx(
+                    out=bank[:],
+                    lhsT=h_codes[:, g, toks].bitcast(FP8X4),
+                    lhsT_scale=h_scales[:, g, toks],
+                    rhs=wo_codes[:, g, :].bitcast(FP8X4),
+                    rhs_scale=wo_scales[:, g, :],
+                    start=(g == 0),
+                    stop=(g == GROUPS - 1),
+                )
+            flush()
+            result = work.tile([P, CH], F32, name="result")
+            copy_out(engine, result[:], bank[:])
+            nc.sync.dma_start(out=out_hbm[toks, :], in_=result[:])
+
+        sobel_step(0)
+        w_step(0, 0, "SV")
+        w_step(0, 1, "SV")
+        w_step(0, 2, "SV")
+        sobel_step(1)
+        s1_step(0, 0, "S", 2)
+        s1_step(0, 1, "V", 2)
+        sobel_step(2)
+        s1_step(0, 2, "S", 2)
+        s1_step(0, 3, "V", 2)
+        sobel_step(3)
+        w_step(1, 0, "SV")
+        s1_step(0, 4, "S", 2)
+        s1_step(0, 5, "V", 2)
+        w_step(1, 1, "SV")
+        s1_step(0, 6, "S", 2)
+        w_step(1, 2, "SV")
+        s1_step(0, 7, "S", 2)
+        products = [(g, r) for g in range(GROUPS) for r in range(4)]
+        for g in (1, 2):
+            for c in range(CHUNKS):
+                s1_step(g, c, "S", 2)
+                if products:
+                    wo_product(*products.pop(0))
+                if c in (1, 3, 5):
+                    w_step(g + 1, c // 2, "SS")
+                if c in (4, 7):
+                    wo_step(2 * (g - 1) + (c == 7), "VV")
+        for c in range(CHUNKS):
+            s1_step(3, c, "S" if c % 2 == 0 else "V", 2 if c < 6 else 1)
+            if c >= 3:
+                s2_step(c - 3, "S" if c % 2 == 1 else "V")
+        flush()
+        for c in (5, 6, 7):
+            s2_step(c, "S" if c % 2 == 0 else "V")

@@ -30,6 +30,7 @@ def tile_nn_kernel(tc, state_grid, W_hidden, W_out_bytes, W_out_scale, out):
     with ExitStack() as ctx:
         keep = ctx.enter_context(tc.tile_pool(name="keep", bufs=1))
         work = ctx.enter_context(tc.tile_pool(name="work", bufs=3))
+        sorting = ctx.enter_context(tc.tile_pool(name="sorting", bufs=5))
         psum = ctx.enter_context(tc.psum_pool(name="psum", bufs=8))
         ctx.enter_context(tc.manual_schedule())
 
@@ -120,11 +121,22 @@ def tile_nn_kernel(tc, state_grid, W_hidden, W_out_bytes, W_out_scale, out):
         wo_scales = keep.tile([P, GROUPS, CH], U8, name="wo_scales", align_bytes=64)
         wo_bf = keep.tile([P, 4, HIDDEN], BF16, name="wo_bf")
 
-        def copy_out(engine, out_ap, in_ap):
-            if engine == "S":
+        load = {"V": 0.0, "S": 0.0}
+
+        def lighter(columns):
+            engine = "S" if load["S"] <= load["V"] else "V"
+            load[engine] += 20 + 0.83 * columns
+            return engine
+
+        def copy_out(out_ap, in_ap, columns):
+            if lighter(columns) == "S":
                 nc.scalar.copy(out=out_ap, in_=in_ap)
             else:
                 nc.vector.tensor_copy(out=out_ap, in_=in_ap)
+
+        def quantize(codes, scales, grouped, columns):
+            load["V"] += 100 + 0.22 * columns
+            nc.vector.quantize_mx(out=codes.bitcast(FP8X4), scales=scales, in_=grouped)
 
         pending = []
 
@@ -136,13 +148,13 @@ def tile_nn_kernel(tc, state_grid, W_hidden, W_out_bytes, W_out_scale, out):
             g12 = work.tile([P, 2, GRID, 4], BF16, name="g12", align_bytes=64)
             g3 = work.tile([P, GRID, 4], BF16, name="g3", align_bytes=64)
             tiles = [
-                (x_nat, 2 * b, 32, "S"),
-                (x_shift, 2 * b, 96, "V"),
-                (x_nat, 2 * b + 1, 160, "S"),
-                (x_shift, 2 * b + 1, None, "V"),
+                (x_nat, 2 * b, 32),
+                (x_shift, 2 * b, 96),
+                (x_nat, 2 * b + 1, 160),
+                (x_shift, 2 * b + 1, None),
             ]
             banks = []
-            for src, slot, first, eng in tiles:
+            for src, slot, first in tiles:
                 bank = new_bank()
                 banks.append(bank)
                 for t in range(4):
@@ -156,34 +168,31 @@ def tile_nn_kernel(tc, state_grid, W_hidden, W_out_bytes, W_out_scale, out):
                     q = 2 * s + u
                     nc.tensor.transpose(xbank[:, q * P : (q + 1) * P], words[:, u::2], ident_f[:])
             flush()
-            for (src, slot, first, eng), bank in zip(tiles, banks):
+            for (src, slot, first), bank in zip(tiles, banks):
                 view = bank[:].rearrange("p (t f n) -> p f n t", t=4, f=2)
                 if first is None:
-                    copy_out(eng, g12[:, :, 224:256, :], view[:, :, 0:32, :])
-                    copy_out(eng, g12[:, :, 0:32, :], view[:, :, 32:64, :])
+                    copy_out(g12[:, :, 224:256, :], view[:, :, 0:32, :], 256)
+                    copy_out(g12[:, :, 0:32, :], view[:, :, 32:64, :], 256)
                 else:
-                    copy_out(eng, g12[:, :, first : first + 64, :], view)
+                    copy_out(g12[:, :, first : first + 64, :], view, 512)
             copy_out(
-                "S",
                 g3[:].bitcast(F32).rearrange("p (s r) u -> p s r u", s=2),
                 xbank[:].rearrange("p (s u r) -> p s r u", s=2, u=2),
+                512,
             )
 
             def quant():
-                nc.vector.quantize_mx(
-                    out=x_codes[:, b, 0:2, :].rearrange("p f n -> p (f n)").bitcast(FP8X4),
-                    scales=x_scales[:, b, 0:2, :].rearrange("p f n -> p (f n)"),
-                    in_=g12[:].rearrange("p f n t -> p (f n t)"),
+                quantize(
+                    x_codes[:, b, 0:2, :].rearrange("p f n -> p (f n)"),
+                    x_scales[:, b, 0:2, :].rearrange("p f n -> p (f n)"),
+                    g12[:].rearrange("p f n t -> p (f n t)"),
+                    2048,
                 )
-                nc.vector.quantize_mx(
-                    out=x_codes[:, b, 2, :].bitcast(FP8X4),
-                    scales=x_scales[:, b, 2, :],
-                    in_=g3[:].rearrange("p n t -> p (n t)"),
-                )
+                quantize(x_codes[:, b, 2, :], x_scales[:, b, 2, :], g3[:].rearrange("p n t -> p (n t)"), 1024)
 
             pending.append(quant)
 
-        def turn_step(sources, codes, scales, engines):
+        def turn_step(sources, codes, scales):
             grouped = work.tile([P, 4, P, 4], BF16, name="grouped", align_bytes=64)
             banks = []
             for h in range(2):
@@ -193,40 +202,63 @@ def tile_nn_kernel(tc, state_grid, W_hidden, W_out_bytes, W_out_scale, out):
                     for u in range(2):
                         q = 2 * c + u
                         nc.tensor.transpose(
-                            bank[:, q * P : (q + 1) * P], sources[2 * h + c][:, u::2], ident_f[:]
+                            bank[:, q * P : (q + 1) * P], sources[2 * h + c][u], ident_f[:]
                         )
             flush()
             for h in range(2):
                 copy_out(
-                    engines[h],
                     grouped[:, 2 * h : 2 * h + 2].bitcast(F32),
                     banks[h][:].rearrange("p (c u r) -> p c r u", c=2, u=2),
+                    512,
                 )
 
             def quant():
-                nc.vector.quantize_mx(
-                    out=codes.bitcast(FP8X4), scales=scales, in_=grouped[:].rearrange("p c r t -> p (c r t)")
-                )
+                quantize(codes, scales, grouped[:].rearrange("p c r t -> p (c r t)"), 2048)
 
             pending.append(quant)
 
-        def w_step(g, k, engines):
-            sources = [w_raw[:, g, t, k * 512 : (k + 1) * 512].bitcast(F32) for t in range(4)]
-            turn_step(sources, w_codes[:, g, k, :], w_scales[:, g, k, :], engines)
+        sorted_words = {}
 
-        def wo_step(g, engines):
-            sources = [wo_bf[:, r, g * 512 : (g + 1) * 512].bitcast(F32) for r in range(4)]
-            turn_step(sources, wo_codes[:, g, :], wo_scales[:, g, :], engines)
+        def sort_words(key, src):
+            dst = sorting.tile([P, 4, 2, P], F32, name="sorted", align_bytes=64)
+            sorted_words[key] = dst
+            load["V"] += 60 + 0.45 * 1024
+            nc.vector.tensor_copy(out=dst[:], in_=src.bitcast(F32).rearrange("p c (j u) -> p c u j", u=2))
+
+        def sort_w(g, k):
+            sort_words((g, k), w_raw[:, g, :, k * 512 : (k + 1) * 512])
+
+        def sort_wo(g):
+            sort_words(g, wo_bf[:, :, g * 512 : (g + 1) * 512])
+
+        def w_step(g, k):
+            if (g, k) in sorted_words:
+                dst = sorted_words[(g, k)]
+                sources = [[dst[:, t, u, :] for u in range(2)] for t in range(4)]
+            else:
+                words = w_raw[:, g, :, k * 512 : (k + 1) * 512].bitcast(F32)
+                sources = [[words[:, t, u::2] for u in range(2)] for t in range(4)]
+            turn_step(sources, w_codes[:, g, k, :], w_scales[:, g, k, :])
+
+        def wo_step(g):
+            if g in sorted_words:
+                dst = sorted_words[g]
+                sources = [[dst[:, r, u, :] for u in range(2)] for r in range(4)]
+            else:
+                words = wo_bf[:, :, g * 512 : (g + 1) * 512].bitcast(F32)
+                sources = [[words[:, r, u::2] for u in range(2)] for r in range(4)]
+            turn_step(sources, wo_codes[:, g, :], wo_scales[:, g, :])
 
         def wo_product(g, r):
             cols = slice(g * 512, (g + 1) * 512)
+            load["V"] += 60 + 0.83 * 512
             nc.vector.tensor_tensor(
                 out=wo_bf[:, r, cols], in0=wo_bytes[:, r, cols].bitcast(FP8), in1=wo_scale[:, cols], op=ALU.mult
             )
 
         hid_tiles = {}
 
-        def s1_step(g, c, engine, width):
+        def s1_step(g, c, width=2):
             b, half = c // 2, c % 2
             toks = slice(half * P, half * P + P)
             bank = new_bank()
@@ -249,7 +281,7 @@ def tile_nn_kernel(tc, state_grid, W_hidden, W_out_bytes, W_out_scale, out):
             hid = hid_tiles[0]
             view = bank[:].rearrange("p (t n) -> p n t", t=4)
             dst = hid[:, j * P : (j + 1) * P, :]
-            if engine == "S":
+            if lighter(512) == "S":
                 nc.scalar.activation(out=dst, in_=view, func=ACT.Relu)
             else:
                 nc.vector.tensor_scalar_max(dst, view, 0.0)
@@ -257,15 +289,41 @@ def tile_nn_kernel(tc, state_grid, W_hidden, W_out_bytes, W_out_scale, out):
                 cols = slice((c + 1 - width) * P, (c + 1) * P)
 
                 def quant():
-                    nc.vector.quantize_mx(
-                        out=h_codes[:, g, cols].bitcast(FP8X4),
-                        scales=h_scales[:, g, cols],
-                        in_=hid[:, 0 : width * P, :].rearrange("p n t -> p (n t)"),
+                    quantize(
+                        h_codes[:, g, cols],
+                        h_scales[:, g, cols],
+                        hid[:, 0 : width * P, :].rearrange("p n t -> p (n t)"),
+                        width * 512,
                     )
 
                 pending.append(quant)
 
-        def s2_step(c, engine):
+        def s2_last(c):
+            toks = slice(c * P, (c + 1) * P)
+            banks = []
+            for n in range(2):
+                cols = slice(n * 256, (n + 1) * 256)
+                bank = new_bank()
+                banks.append(bank)
+                for g in range(GROUPS):
+                    nc.tensor.matmul_mx(
+                        out=bank[:, 0:256],
+                        lhsT=h_codes[:, g, toks].bitcast(FP8X4),
+                        lhsT_scale=h_scales[:, g, toks],
+                        rhs=wo_codes[:, g, cols].bitcast(FP8X4),
+                        rhs_scale=wo_scales[:, g, cols],
+                        start=(g == 0),
+                        stop=(g == GROUPS - 1),
+                    )
+            for n in range(2):
+                half = work.tile([P, 256], F32, name="half_result")
+                if n == 0:
+                    nc.scalar.copy(out=half[:], in_=banks[n][:, 0:256])
+                else:
+                    nc.vector.tensor_copy(out=half[:], in_=banks[n][:, 0:256])
+                nc.sync.dma_start(out=out_hbm[toks, n * 256 : (n + 1) * 256], in_=half[:])
+
+        def s2_step(c):
             toks = slice(c * P, (c + 1) * P)
             bank = new_bank()
             for g in range(GROUPS):
@@ -280,41 +338,58 @@ def tile_nn_kernel(tc, state_grid, W_hidden, W_out_bytes, W_out_scale, out):
                 )
             flush()
             result = work.tile([P, CH], F32, name="result")
-            copy_out(engine, result[:], bank[:])
+            copy_out(result[:], bank[:], 512)
             nc.sync.dma_start(out=out_hbm[toks, :], in_=result[:])
 
+        warm_bank = new_bank()
+        for i in range(12):
+            nc.tensor.matmul(warm_bank[:, 0:P], ident_b[:], ident_b[:], start=True, stop=True)
         sobel_step(0)
-        w_step(0, 0, "SV")
-        w_step(0, 1, "SV")
-        w_step(0, 2, "SV")
+        w_step(0, 0)
+        w_step(0, 1)
+        w_step(0, 2)
         sobel_step(1)
-        s1_step(0, 0, "S", 2)
-        s1_step(0, 1, "V", 2)
+        s1_step(0, 0)
+        s1_step(0, 1)
         sobel_step(2)
-        s1_step(0, 2, "S", 2)
-        s1_step(0, 3, "V", 2)
+        s1_step(0, 2)
+        s1_step(0, 3)
         sobel_step(3)
-        w_step(1, 0, "SV")
-        s1_step(0, 4, "S", 2)
-        s1_step(0, 5, "V", 2)
-        w_step(1, 1, "SV")
-        s1_step(0, 6, "S", 2)
-        w_step(1, 2, "SV")
-        s1_step(0, 7, "S", 2)
+        sort_w(1, 0)
+        s1_step(0, 4)
+        sort_w(1, 1)
+        s1_step(0, 5)
+        sort_w(1, 2)
+        w_step(1, 0)
+        w_step(1, 1)
+        s1_step(0, 6)
+        w_step(1, 2)
+        s1_step(0, 7)
         products = [(g, r) for g in range(GROUPS) for r in range(4)]
         for g in (1, 2):
             for c in range(CHUNKS):
-                s1_step(g, c, "S", 2)
-                if products:
-                    wo_product(*products.pop(0))
-                if c in (1, 3, 5):
-                    w_step(g + 1, c // 2, "SS")
-                if c in (4, 7):
-                    wo_step(2 * (g - 1) + (c == 7), "VV")
+                s1_step(g, c)
+                wo_product(*products.pop(0))
+                if c in (0, 1, 2):
+                    sort_w(g + 1, c)
+                if c == 3:
+                    w_step(g + 1, 0)
+                    w_step(g + 1, 1)
+                    sort_wo(2 * g - 2)
+                if c == 5:
+                    w_step(g + 1, 2)
+                    wo_step(2 * g - 2)
+                if c == 7:
+                    sort_wo(2 * g - 1)
+                if c == 1 and g == 2:
+                    wo_step(1)
         for c in range(CHUNKS):
-            s1_step(3, c, "S" if c % 2 == 0 else "V", 2 if c < 6 else 1)
+            s1_step(3, c, 2 if c < 6 else 1)
+            if c == 1:
+                wo_step(3)
             if c >= 3:
-                s2_step(c - 3, "S" if c % 2 == 1 else "V")
+                s2_step(c - 3)
         flush()
-        for c in (5, 6, 7):
-            s2_step(c, "S" if c % 2 == 0 else "V")
+        s2_step(5)
+        s2_step(6)
+        s2_last(7)

@@ -30,7 +30,7 @@ def tile_nn_kernel(tc, state_grid, W_hidden, W_out_bytes, W_out_scale, out):
     with ExitStack() as ctx:
         keep = ctx.enter_context(tc.tile_pool(name="keep", bufs=1))
         work = ctx.enter_context(tc.tile_pool(name="work", bufs=3))
-        sorting = ctx.enter_context(tc.tile_pool(name="sorting", bufs=5))
+        sorting = ctx.enter_context(tc.tile_pool(name="sorting", bufs=4))
         psum = ctx.enter_context(tc.psum_pool(name="psum", bufs=8))
         ctx.enter_context(tc.manual_schedule())
 
@@ -47,11 +47,16 @@ def tile_nn_kernel(tc, state_grid, W_hidden, W_out_bytes, W_out_scale, out):
 
         def load_x(b):
             t0 = b * GRID
-            nc.sync.dma_start(
-                out=x_nat[:, 2 * b : 2 * b + 2, :],
-                in_=x_hbm[t0 : t0 + GRID, :].rearrange("(s p) c -> p s c", p=P),
-            )
-            nc.sync.dma_start(out=x_shift[:, 2 * b, :], in_=x_hbm[t0 + 64 : t0 + 192, :])
+            if b == 0:
+                nc.sync.dma_start(out=x_nat[:, 0, :], in_=x_hbm[0:P, :])
+                nc.sync.dma_start(out=x_shift[:, 0, :], in_=x_hbm[64:192, :])
+                nc.sync.dma_start(out=x_nat[:, 1, :], in_=x_hbm[P:GRID, :])
+            else:
+                nc.sync.dma_start(
+                    out=x_nat[:, 2 * b : 2 * b + 2, :],
+                    in_=x_hbm[t0 : t0 + GRID, :].rearrange("(s p) c -> p s c", p=P),
+                )
+                nc.sync.dma_start(out=x_shift[:, 2 * b, :], in_=x_hbm[t0 + 64 : t0 + 192, :])
             nc.sync.dma_start(out=x_shift[0:64, 2 * b + 1, :], in_=x_hbm[t0 + 192 : t0 + 256, :])
             nc.sync.dma_start(out=x_shift[64:128, 2 * b + 1, :], in_=x_hbm[t0 : t0 + 64, :])
 
@@ -135,7 +140,7 @@ def tile_nn_kernel(tc, state_grid, W_hidden, W_out_bytes, W_out_scale, out):
                 nc.vector.tensor_copy(out=out_ap, in_=in_ap)
 
         def quantize(codes, scales, grouped, columns):
-            load["V"] += 100 + 0.22 * columns
+            load["V"] += 40 + 0.22 * columns
             nc.vector.quantize_mx(out=codes.bitcast(FP8X4), scales=scales, in_=grouped)
 
         pending = []
@@ -143,6 +148,17 @@ def tile_nn_kernel(tc, state_grid, W_hidden, W_out_bytes, W_out_scale, out):
         def flush():
             while pending:
                 pending.pop(0)()
+
+        sorted_x = {}
+
+        def sort_x(b):
+            dst = work.tile([P, 2, 2, P], F32, name="sorted_x", align_bytes=64)
+            sorted_x[b] = dst
+            load["V"] += 20 + 0.45 * 512
+            nc.vector.tensor_copy(
+                out=dst[:],
+                in_=x_nat[:, 2 * b : 2 * b + 2, :].bitcast(F32).rearrange("p s (j u) -> p s u j", u=2),
+            )
 
         def sobel_step(b):
             g12 = work.tile([P, 2, GRID, 4], BF16, name="g12", align_bytes=64)
@@ -163,10 +179,13 @@ def tile_nn_kernel(tc, state_grid, W_hidden, W_out_bytes, W_out_scale, out):
                     )
             xbank = new_bank()
             for s in range(2):
-                words = x_nat[:, 2 * b + s, :].bitcast(F32)
                 for u in range(2):
                     q = 2 * s + u
-                    nc.tensor.transpose(xbank[:, q * P : (q + 1) * P], words[:, u::2], ident_f[:])
+                    if b in sorted_x:
+                        words = sorted_x[b][:, s, u, :]
+                    else:
+                        words = x_nat[:, 2 * b + s, :].bitcast(F32)[:, u::2]
+                    nc.tensor.transpose(xbank[:, q * P : (q + 1) * P], words, ident_f[:])
             flush()
             for (src, slot, first), bank in zip(tiles, banks):
                 view = bank[:].rearrange("p (t f n) -> p f n t", t=4, f=2)
@@ -222,7 +241,7 @@ def tile_nn_kernel(tc, state_grid, W_hidden, W_out_bytes, W_out_scale, out):
         def sort_words(key, src):
             dst = sorting.tile([P, 4, 2, P], F32, name="sorted", align_bytes=64)
             sorted_words[key] = dst
-            load["V"] += 60 + 0.45 * 1024
+            load["V"] += 20 + 0.45 * 1024
             nc.vector.tensor_copy(out=dst[:], in_=src.bitcast(F32).rearrange("p c (j u) -> p c u j", u=2))
 
         def sort_w(g, k):
@@ -251,7 +270,7 @@ def tile_nn_kernel(tc, state_grid, W_hidden, W_out_bytes, W_out_scale, out):
 
         def wo_product(g, r):
             cols = slice(g * 512, (g + 1) * 512)
-            load["V"] += 60 + 0.83 * 512
+            load["V"] += 20 + 0.83 * 512
             nc.vector.tensor_tensor(
                 out=wo_bf[:, r, cols], in0=wo_bytes[:, r, cols].bitcast(FP8), in1=wo_scale[:, cols], op=ALU.mult
             )
@@ -275,10 +294,11 @@ def tile_nn_kernel(tc, state_grid, W_hidden, W_out_bytes, W_out_scale, out):
                     )
             flush()
             j = c % width
-            if j == 0:
+            key = (g, c // width, width)
+            if key not in hid_tiles:
                 hid = work.tile([P, 2 * P, 4], BF16, name="hid", align_bytes=64)
-                hid_tiles[0] = hid
-            hid = hid_tiles[0]
+                hid_tiles[key] = hid
+            hid = hid_tiles[key]
             view = bank[:].rearrange("p (t n) -> p n t", t=4)
             dst = hid[:, j * P : (j + 1) * P, :]
             if lighter(512) == "S":
@@ -298,6 +318,41 @@ def tile_nn_kernel(tc, state_grid, W_hidden, W_out_bytes, W_out_scale, out):
 
                 pending.append(quant)
 
+        def s1_wide(g, b):
+            hid = work.tile([P, 2 * P, 4], BF16, name="hid", align_bytes=64)
+            banks = []
+            for h in range(2):
+                bank = new_bank()
+                banks.append(bank)
+                for i in range(2):
+                    t = 2 * h + i
+                    for k in range(3):
+                        nc.tensor.matmul_mx(
+                            out=bank[:, i * GRID : (i + 1) * GRID],
+                            lhsT=w_codes[:, g, k, t * P : (t + 1) * P].bitcast(FP8X4),
+                            lhsT_scale=w_scales[:, g, k, t * P : (t + 1) * P],
+                            rhs=x_codes[:, b, k, :].bitcast(FP8X4),
+                            rhs_scale=x_scales[:, b, k, :],
+                            start=(k == 0),
+                            stop=(k == 2),
+                        )
+            flush()
+            for h in range(2):
+                view = banks[h][:].rearrange("p (t n) -> p n t", t=2)
+                dst = hid[:, :, 2 * h : 2 * h + 2]
+                if lighter(768) == "S":
+                    nc.scalar.activation(out=dst, in_=view, func=ACT.Relu)
+                else:
+                    nc.vector.tensor_scalar_max(dst, view, 0.0)
+            cols = slice(b * GRID, (b + 1) * GRID)
+
+            def quant():
+                quantize(
+                    h_codes[:, g, cols], h_scales[:, g, cols], hid[:].rearrange("p n t -> p (n t)"), 1024
+                )
+
+            pending.append(quant)
+
         def s2_last(c):
             toks = slice(c * P, (c + 1) * P)
             banks = []
@@ -316,7 +371,7 @@ def tile_nn_kernel(tc, state_grid, W_hidden, W_out_bytes, W_out_scale, out):
                         stop=(g == GROUPS - 1),
                     )
             for n in range(2):
-                half = work.tile([P, 256], F32, name="half_result")
+                half = work.tile([P, 256], F32, name="sorted_x", align_bytes=64)
                 if n == 0:
                     nc.scalar.copy(out=half[:], in_=banks[n][:, 0:256])
                 else:
@@ -346,50 +401,80 @@ def tile_nn_kernel(tc, state_grid, W_hidden, W_out_bytes, W_out_scale, out):
             nc.tensor.matmul(warm_bank[:, 0:P], ident_b[:], ident_b[:], start=True, stop=True)
         sobel_step(0)
         w_step(0, 0)
+        sort_x(1)
         w_step(0, 1)
+        sort_x(2)
         w_step(0, 2)
         sobel_step(1)
-        s1_step(0, 0)
-        s1_step(0, 1)
         sobel_step(2)
-        s1_step(0, 2)
-        s1_step(0, 3)
-        sobel_step(3)
+        s1_step(0, 0)
         sort_w(1, 0)
-        s1_step(0, 4)
+        sobel_step(3)
         sort_w(1, 1)
-        s1_step(0, 5)
-        sort_w(1, 2)
+        s1_wide(0, 1)
+        wo_product(0, 0)
         w_step(1, 0)
         w_step(1, 1)
-        s1_step(0, 6)
+        wo_product(0, 1)
         w_step(1, 2)
-        s1_step(0, 7)
-        products = [(g, r) for g in range(GROUPS) for r in range(4)]
-        for g in (1, 2):
-            for c in range(CHUNKS):
-                s1_step(g, c)
-                wo_product(*products.pop(0))
-                if c in (0, 1, 2):
-                    sort_w(g + 1, c)
-                if c == 3:
-                    w_step(g + 1, 0)
-                    w_step(g + 1, 1)
-                    sort_wo(2 * g - 2)
-                if c == 5:
-                    w_step(g + 1, 2)
-                    wo_step(2 * g - 2)
-                if c == 7:
-                    sort_wo(2 * g - 1)
-                if c == 1 and g == 2:
-                    wo_step(1)
-        for c in range(CHUNKS):
-            s1_step(3, c, 2 if c < 6 else 1)
-            if c == 1:
-                wo_step(3)
-            if c >= 3:
-                s2_step(c - 3)
-        flush()
+        s1_step(0, 1)
+        sort_w(2, 0)
+        s1_wide(0, 2)
+        s1_wide(0, 3)
+        sort_w(2, 1)
+        s1_step(1, 0)
+        s1_step(1, 1)
+        wo_product(0, 2)
+        wo_product(0, 3)
+        sort_w(2, 2)
+        s1_wide(1, 1)
+        wo_product(1, 0)
+        s1_step(1, 4)
+        wo_product(1, 1)
+        wo_product(1, 2)
+        w_step(2, 0)
+        w_step(2, 1)
+        w_step(2, 2)
+        wo_step(0)
+        sort_w(3, 0)
+        s1_step(1, 5)
+        s1_step(1, 6)
+        s1_step(1, 7)
+        wo_product(1, 3)
+        sort_w(3, 1)
+        s1_step(2, 0)
+        s1_wide(2, 1)
+        wo_product(2, 0)
+        sort_w(3, 2)
+        s1_step(2, 1)
+        wo_product(2, 1)
+        wo_product(2, 2)
+        w_step(3, 0)
+        wo_product(2, 3)
+        w_step(3, 1)
+        sort_wo(1)
+        w_step(3, 2)
+        s1_wide(2, 2)
+        wo_product(3, 0)
+        sort_wo(2)
+        wo_product(3, 1)
+        wo_product(3, 2)
+        wo_product(3, 3)
+        sort_wo(3)
+        s1_wide(2, 3)
+        s1_wide(3, 0)
+        s1_step(3, 2)
+        wo_step(1)
+        wo_step(2)
+        wo_step(3)
+        s1_step(3, 3)
+        s1_wide(3, 2)
+        s1_wide(3, 3)
+        s2_step(0)
+        s2_step(1)
+        s2_step(2)
+        s2_step(3)
+        s2_step(4)
         s2_step(5)
         s2_step(6)
         s2_last(7)

@@ -72,13 +72,13 @@ def tile_nn_kernel(tc, state_grid, W_hidden, W_out_bytes, W_out_scale, out):
         load_w_pass(0, 2)
         load_x(1)
         load_x(2)
-        load_x(3)
         nc.sync.dma_start(out=w_raw[:, 1], in_=w_hbm[1])
-        nc.sync.dma_start(out=wo_bytes[:], in_=W_out_bytes.rearrange("(r p) k -> p r k", p=P))
+        nc.sync.dma_start(out=w_raw[:, 2], in_=w_hbm[2])
+        load_x(3)
         nc.sync.dma_start(
             out=wo_scale[:], in_=W_out_scale.rearrange("o k -> (o k)").partition_broadcast(P)
         )
-        nc.sync.dma_start(out=w_raw[:, 2], in_=w_hbm[2])
+        nc.sync.dma_start(out=wo_bytes[:], in_=W_out_bytes.rearrange("(r p) k -> p r k", p=P))
         nc.sync.dma_start(out=w_raw[:, 3], in_=w_hbm[3])
 
         warm = keep.tile([P, 1], F32, name="warm")
@@ -399,81 +399,80 @@ def tile_nn_kernel(tc, state_grid, W_hidden, W_out_bytes, W_out_scale, out):
         warm_bank = new_bank()
         for i in range(12):
             nc.tensor.matmul(warm_bank[:, 0:P], ident_b[:], ident_b[:], start=True, stop=True)
+        sort_x(0)
         sobel_step(0)
         w_step(0, 0)
-        sort_x(1)
         w_step(0, 1)
-        sort_x(2)
+        sort_x(1)
         w_step(0, 2)
         sobel_step(1)
         sobel_step(2)
-        s1_step(0, 0)
+        s1_wide(0, 0)
         sort_w(1, 0)
-        sobel_step(3)
         sort_w(1, 1)
+        sort_w(1, 2)
         s1_wide(0, 1)
-        wo_product(0, 0)
+        s1_step(0, 4)
         w_step(1, 0)
         w_step(1, 1)
-        wo_product(0, 1)
-        w_step(1, 2)
-        s1_step(0, 1)
         sort_w(2, 0)
-        s1_wide(0, 2)
-        s1_wide(0, 3)
-        sort_w(2, 1)
-        s1_step(1, 0)
-        s1_step(1, 1)
-        wo_product(0, 2)
-        wo_product(0, 3)
-        sort_w(2, 2)
-        s1_wide(1, 1)
-        wo_product(1, 0)
-        s1_step(1, 4)
-        wo_product(1, 1)
-        wo_product(1, 2)
+        w_step(1, 2)
+        sobel_step(3)
         w_step(2, 0)
-        w_step(2, 1)
-        w_step(2, 2)
-        wo_step(0)
-        sort_w(3, 0)
-        s1_step(1, 5)
-        s1_step(1, 6)
-        s1_step(1, 7)
-        wo_product(1, 3)
+        s1_step(0, 5)
+        sort_w(2, 1)
+        s1_wide(1, 0)
+        wo_product(0, 0)
+        s1_step(1, 2)
+        sort_w(2, 2)
+        wo_product(0, 1)
+        wo_product(0, 2)
         sort_w(3, 1)
-        s1_step(2, 0)
-        s1_wide(2, 1)
-        wo_product(2, 0)
+        s1_wide(0, 3)
         sort_w(3, 2)
-        s1_step(2, 1)
+        wo_product(0, 3)
+        s1_step(1, 3)
+        wo_product(1, 0)
+        w_step(2, 1)
+        w_step(3, 0)
+        w_step(3, 1)
+        w_step(2, 2)
+        wo_product(1, 1)
+        w_step(3, 2)
+        wo_product(1, 2)
+        wo_product(1, 3)
+        s1_wide(1, 2)
+        wo_product(2, 0)
         wo_product(2, 1)
         wo_product(2, 2)
-        w_step(3, 0)
         wo_product(2, 3)
-        w_step(3, 1)
-        sort_wo(1)
-        w_step(3, 2)
-        s1_wide(2, 2)
+        s1_wide(1, 3)
         wo_product(3, 0)
+        sort_wo(0)
+        s1_wide(2, 0)
+        sort_wo(1)
+        s1_wide(2, 1)
         sort_wo(2)
+        s1_step(2, 4)
         wo_product(3, 1)
+        s1_step(2, 5)
         wo_product(3, 2)
         wo_product(3, 3)
+        s1_step(3, 0)
         sort_wo(3)
-        s1_wide(2, 3)
-        s1_wide(3, 0)
-        s1_step(3, 2)
+        s1_wide(3, 1)
+        s1_step(3, 1)
+        wo_step(0)
         wo_step(1)
         wo_step(2)
         wo_step(3)
-        s1_step(3, 3)
         s1_wide(3, 2)
         s1_wide(3, 3)
         s2_step(0)
         s2_step(1)
         s2_step(2)
         s2_step(3)
+        s1_wide(2, 3)
         s2_step(4)
         s2_step(5)
         s2_step(6)

from contextlib import ExitStack

import concourse.mybir as mybir
from concourse.masks import make_identity

F32 = mybir.dt.float32
BF16 = mybir.dt.bfloat16
U32 = mybir.dt.uint32
U8 = mybir.dt.uint8
FP8 = mybir.dt.float8_e4m3fn
FP8X4 = mybir.dt.float8_e4m3fn_x4
ALU = mybir.AluOpType
ACT = mybir.ActivationFunctionType

P = 128
BATCH, HEIGHT, WIDTH, CH, HIDDEN = 4, 16, 16, 512, 2048
GRID = HEIGHT * WIDTH
TOKENS = BATCH * GRID
PASSES1 = 3 * CH // 512
GROUPS = HIDDEN // 512
CHUNKS = TOKENS // P
FLOPS = 2 * TOKENS * 3 * CH * HIDDEN + 2 * TOKENS * HIDDEN * CH


def tile_nn_kernel(tc, state_grid, W_hidden, W_out_bytes, W_out_scale, out):
    nc = tc.nc
    x_hbm = state_grid.rearrange("b i j c -> (b i j) c")
    out_hbm = out.rearrange("b i j c -> (b i j) c")

    with ExitStack() as ctx:
        keep = ctx.enter_context(tc.tile_pool(name="keep", bufs=1))
        work = ctx.enter_context(tc.tile_pool(name="work", bufs=3))
        sorting = ctx.enter_context(tc.tile_pool(name="sorting", bufs=4))
        psum = ctx.enter_context(tc.psum_pool(name="psum", bufs=8))
        ctx.enter_context(tc.manual_schedule())

        def new_bank():
            bank = psum.tile([P, 512], F32, name="bank")
            return bank

        x_nat = keep.tile([P, 2 * BATCH, CH], BF16, name="x_nat")
        x_shift = keep.tile([P, 2 * BATCH, CH], BF16, name="x_shift")
        w_raw = keep.tile([P, GROUPS, 4, 3 * CH], BF16, name="w_raw")
        wo_bytes = keep.tile([P, 4, HIDDEN], U8, name="wo_bytes")
        wo_scale = keep.tile([P, HIDDEN], F32, name="wo_scale")
        w_hbm = W_hidden.rearrange("(g m t) k -> g m t k", m=P, t=4)

        def load_x(b):
            t0 = b * GRID
            if b == 0:
                nc.sync.dma_start(out=x_nat[:, 0, :], in_=x_hbm[0:P, :])
                nc.sync.dma_start(out=x_shift[:, 0, :], in_=x_hbm[64:192, :])
                nc.sync.dma_start(out=x_nat[:, 1, :], in_=x_hbm[P:GRID, :])
            else:
                nc.sync.dma_start(
                    out=x_nat[:, 2 * b : 2 * b + 2, :],
                    in_=x_hbm[t0 : t0 + GRID, :].rearrange("(s p) c -> p s c", p=P),
                )
                nc.sync.dma_start(out=x_shift[:, 2 * b, :], in_=x_hbm[t0 + 64 : t0 + 192, :])
            nc.sync.dma_start(out=x_shift[0:64, 2 * b + 1, :], in_=x_hbm[t0 + 192 : t0 + 256, :])
            nc.sync.dma_start(out=x_shift[64:128, 2 * b + 1, :], in_=x_hbm[t0 : t0 + 64, :])

        def load_w_pass(g, k):
            nc.sync.dma_start(
                out=w_raw[:, g, :, k * 512 : (k + 1) * 512],
                in_=w_hbm[g][:, :, k * 512 : (k + 1) * 512],
            )

        load_x(0)
        load_w_pass(0, 0)
        load_w_pass(0, 1)
        load_w_pass(0, 2)
        load_x(1)
        load_x(2)
        nc.sync.dma_start(out=w_raw[:, 1], in_=w_hbm[1])
        nc.sync.dma_start(out=w_raw[:, 2], in_=w_hbm[2])
        load_x(3)
        nc.sync.dma_start(
            out=wo_scale[:], in_=W_out_scale.rearrange("o k -> (o k)").partition_broadcast(P)
        )
        nc.sync.dma_start(out=wo_bytes[:], in_=W_out_bytes.rearrange("(r p) k -> p r k", p=P))
        nc.sync.dma_start(out=w_raw[:, 3], in_=w_hbm[3])

        warm = keep.tile([P, 1], F32, name="warm")
        nc.vector.memset(warm[:], 0.0)
        nc.scalar.activation(out=warm[:], in_=warm[:], func=ACT.Relu)

        ident_b = keep.tile([P, P], BF16, name="ident_b")
        ident_f = keep.tile([P, P], F32, name="ident_f")
        make_identity(nc, ident_b[:])
        nc.vector.tensor_copy(out=ident_f[:], in_=ident_b[:])
        padded = keep.tile([P, 8, 18], BF16, name="padded")
        ident_rows = ident_b[:].rearrange("p (i j) -> p i j", j=16)
        nc.vector.tensor_copy(out=padded[:, :, 1:17], in_=ident_rows)
        nc.vector.tensor_copy(out=padded[:, :, 0:1], in_=ident_rows[:, :, 15:16])
        nc.vector.tensor_copy(out=padded[:, :, 17:18], in_=ident_rows[:, :, 0:1])
        diff = keep.tile([P, P], BF16, name="diff")
        smooth = keep.tile([P, P], BF16, name="smooth")
        part = keep.tile([P, P], BF16, name="part")
        sobel = keep.tile([P, 2, 64], BF16, name="sobel")
        rows16 = "p (i j) -> p i j"
        nc.vector.tensor_tensor(
            out=diff[:].rearrange(rows16, j=16), in0=padded[:, :, 2:18], in1=padded[:, :, 0:16], op=ALU.subtract
        )
        nc.vector.tensor_tensor(
            out=part[:].rearrange(rows16, j=16), in0=padded[:, :, 2:18], in1=padded[:, :, 0:16], op=ALU.add
        )
        nc.vector.scalar_tensor_tensor(
            out=smooth[:], in0=ident_b[:], scalar=2.0, in1=part[:], op0=ALU.mult, op1=ALU.add
        )
        around = keep.tile([P, 64], BF16, name="around")
        nc.vector.tensor_tensor(out=around[:], in0=diff[:, 16:80], in1=diff[:, 48:112], op=ALU.add)
        nc.vector.scalar_tensor_tensor(
            out=sobel[:, 0, :], in0=diff[:, 32:96], scalar=2.0, in1=around[:], op0=ALU.mult, op1=ALU.add
        )
        nc.vector.tensor_tensor(out=sobel[:, 1, :], in0=smooth[:, 48:112], in1=smooth[:, 16:80], op=ALU.subtract)
        sobel_cols = sobel[:].rearrange("p f n -> p (f n)")

        x_codes = keep.tile([P, BATCH, 3, GRID], U32, name="x_codes", align_bytes=64)
        x_scales = keep.tile([P, BATCH, 3, GRID], U8, name="x_scales", align_bytes=64)
        w_codes = keep.tile([P, GROUPS, 3, 512], U32, name="w_codes", align_bytes=64)
        w_scales = keep.tile([P, GROUPS, 3, 512], U8, name="w_scales", align_bytes=64)
        h_codes = keep.tile([P, GROUPS, TOKENS], U32, name="h_codes", align_bytes=64)
        h_scales = keep.tile([P, GROUPS, TOKENS], U8, name="h_scales", align_bytes=64)
        wo_codes = keep.tile([P, GROUPS, CH], U32, name="wo_codes", align_bytes=64)
        wo_scales = keep.tile([P, GROUPS, CH], U8, name="wo_scales", align_bytes=64)
        wo_bf = keep.tile([P, 4, HIDDEN], BF16, name="wo_bf")

        load = {"V": 0.0, "S": 0.0}

        def lighter(columns):
            engine = "S" if load["S"] <= load["V"] else "V"
            load[engine] += 20 + 0.83 * columns
            return engine

        def copy_out(out_ap, in_ap, columns):
            if lighter(columns) == "S":
                nc.scalar.copy(out=out_ap, in_=in_ap)
            else:
                nc.vector.tensor_copy(out=out_ap, in_=in_ap)

        def quantize(codes, scales, grouped, columns):
            load["V"] += 40 + 0.22 * columns
            nc.vector.quantize_mx(out=codes.bitcast(FP8X4), scales=scales, in_=grouped)

        pending = []

        def flush():
            while pending:
                pending.pop(0)()

        sorted_x = {}

        def sort_x(b):
            dst = work.tile([P, 2, 2, P], F32, name="sorted_x", align_bytes=64)
            sorted_x[b] = dst
            load["V"] += 20 + 0.45 * 512
            nc.vector.tensor_copy(
                out=dst[:],
                in_=x_nat[:, 2 * b : 2 * b + 2, :].bitcast(F32).rearrange("p s (j u) -> p s u j", u=2),
            )

        def sobel_step(b):
            g12 = work.tile([P, 2, GRID, 4], BF16, name="g12", align_bytes=64)
            g3 = work.tile([P, GRID, 4], BF16, name="g3", align_bytes=64)
            tiles = [
                (x_nat, 2 * b, 32),
                (x_shift, 2 * b, 96),
                (x_nat, 2 * b + 1, 160),
                (x_shift, 2 * b + 1, None),
            ]
            banks = []
            for src, slot, first in tiles:
                bank = new_bank()
                banks.append(bank)
                for t in range(4):
                    nc.tensor.matmul(
                        bank[:, t * P : (t + 1) * P], src[:, slot, t::4], sobel_cols, start=True, stop=True
                    )
            xbank = new_bank()
            for s in range(2):
                for u in range(2):
                    q = 2 * s + u
                    if b in sorted_x:
                        words = sorted_x[b][:, s, u, :]
                    else:
                        words = x_nat[:, 2 * b + s, :].bitcast(F32)[:, u::2]
                    nc.tensor.transpose(xbank[:, q * P : (q + 1) * P], words, ident_f[:])
            flush()
            for (src, slot, first), bank in zip(tiles, banks):
                view = bank[:].rearrange("p (t f n) -> p f n t", t=4, f=2)
                if first is None:
                    copy_out(g12[:, :, 224:256, :], view[:, :, 0:32, :], 256)
                    copy_out(g12[:, :, 0:32, :], view[:, :, 32:64, :], 256)
                else:
                    copy_out(g12[:, :, first : first + 64, :], view, 512)
            copy_out(
                g3[:].bitcast(F32).rearrange("p (s r) u -> p s r u", s=2),
                xbank[:].rearrange("p (s u r) -> p s r u", s=2, u=2),
                512,
            )

            def quant():
                quantize(
                    x_codes[:, b, 0:2, :].rearrange("p f n -> p (f n)"),
                    x_scales[:, b, 0:2, :].rearrange("p f n -> p (f n)"),
                    g12[:].rearrange("p f n t -> p (f n t)"),
                    2048,
                )
                quantize(x_codes[:, b, 2, :], x_scales[:, b, 2, :], g3[:].rearrange("p n t -> p (n t)"), 1024)

            pending.append(quant)

        def turn_step(sources, codes, scales):
            grouped = work.tile([P, 4, P, 4], BF16, name="grouped", align_bytes=64)
            banks = []
            for h in range(2):
                bank = new_bank()
                banks.append(bank)
                for c in range(2):
                    for u in range(2):
                        q = 2 * c + u
                        nc.tensor.transpose(
                            bank[:, q * P : (q + 1) * P], sources[2 * h + c][u], ident_f[:]
                        )
            flush()
            for h in range(2):
                copy_out(
                    grouped[:, 2 * h : 2 * h + 2].bitcast(F32),
                    banks[h][:].rearrange("p (c u r) -> p c r u", c=2, u=2),
                    512,
                )

            def quant():
                quantize(codes, scales, grouped[:].rearrange("p c r t -> p (c r t)"), 2048)

            pending.append(quant)

        sorted_words = {}

        def sort_words(key, src):
            dst = sorting.tile([P, 4, 2, P], F32, name="sorted", align_bytes=64)
            sorted_words[key] = dst
            load["V"] += 20 + 0.45 * 1024
            nc.vector.tensor_copy(out=dst[:], in_=src.bitcast(F32).rearrange("p c (j u) -> p c u j", u=2))

        def sort_w(g, k):
            sort_words((g, k), w_raw[:, g, :, k * 512 : (k + 1) * 512])

        def sort_wo(g):
            sort_words(g, wo_bf[:, :, g * 512 : (g + 1) * 512])

        def w_step(g, k):
            if (g, k) in sorted_words:
                dst = sorted_words[(g, k)]
                sources = [[dst[:, t, u, :] for u in range(2)] for t in range(4)]
            else:
                words = w_raw[:, g, :, k * 512 : (k + 1) * 512].bitcast(F32)
                sources = [[words[:, t, u::2] for u in range(2)] for t in range(4)]
            turn_step(sources, w_codes[:, g, k, :], w_scales[:, g, k, :])

        def wo_step(g):
            if g in sorted_words:
                dst = sorted_words[g]
                sources = [[dst[:, r, u, :] for u in range(2)] for r in range(4)]
            else:
                words = wo_bf[:, :, g * 512 : (g + 1) * 512].bitcast(F32)
                sources = [[words[:, r, u::2] for u in range(2)] for r in range(4)]
            turn_step(sources, wo_codes[:, g, :], wo_scales[:, g, :])

        def wo_product(g, r):
            cols = slice(g * 512, (g + 1) * 512)
            load["V"] += 20 + 0.83 * 512
            nc.vector.tensor_tensor(
                out=wo_bf[:, r, cols], in0=wo_bytes[:, r, cols].bitcast(FP8), in1=wo_scale[:, cols], op=ALU.mult
            )

        hid_tiles = {}

        def s1_step(g, c, width=2):
            b, half = c // 2, c % 2
            toks = slice(half * P, half * P + P)
            bank = new_bank()
            for t in range(4):
                for k in range(3):
                    nc.tensor.matmul_mx(
                        out=bank[:, t * P : (t + 1) * P],
                        lhsT=w_codes[:, g, k, t * P : (t + 1) * P].bitcast(FP8X4),
                        lhsT_scale=w_scales[:, g, k, t * P : (t + 1) * P],
                        rhs=x_codes[:, b, k, toks].bitcast(FP8X4),
                        rhs_scale=x_scales[:, b, k, toks],
                        start=(k == 0),
                        stop=(k == 2),
                    )
            flush()
            j = c % width
            key = (g, c // width, width)
            if key not in hid_tiles:
                hid = work.tile([P, 2 * P, 4], BF16, name="hid", align_bytes=64)
                hid_tiles[key] = hid
            hid = hid_tiles[key]
            view = bank[:].rearrange("p (t n) -> p n t", t=4)
            dst = hid[:, j * P : (j + 1) * P, :]
            if lighter(512) == "S":
                nc.scalar.activation(out=dst, in_=view, func=ACT.Relu)
            else:
                nc.vector.tensor_scalar_max(dst, view, 0.0)
            if j == width - 1:
                cols = slice((c + 1 - width) * P, (c + 1) * P)

                def quant():
                    quantize(
                        h_codes[:, g, cols],
                        h_scales[:, g, cols],
                        hid[:, 0 : width * P, :].rearrange("p n t -> p (n t)"),
                        width * 512,
                    )

                pending.append(quant)

        def s1_wide(g, b):
            hid = work.tile([P, 2 * P, 4], BF16, name="hid", align_bytes=64)
            banks = []
            for h in range(2):
                bank = new_bank()
                banks.append(bank)
                for i in range(2):
                    t = 2 * h + i
                    for k in range(3):
                        nc.tensor.matmul_mx(
                            out=bank[:, i * GRID : (i + 1) * GRID],
                            lhsT=w_codes[:, g, k, t * P : (t + 1) * P].bitcast(FP8X4),
                            lhsT_scale=w_scales[:, g, k, t * P : (t + 1) * P],
                            rhs=x_codes[:, b, k, :].bitcast(FP8X4),
                            rhs_scale=x_scales[:, b, k, :],
                            start=(k == 0),
                            stop=(k == 2),
                        )
            flush()
            for h in range(2):
                view = banks[h][:].rearrange("p (t n) -> p n t", t=2)
                dst = hid[:, :, 2 * h : 2 * h + 2]
                if lighter(768) == "S":
                    nc.scalar.activation(out=dst, in_=view, func=ACT.Relu)
                else:
                    nc.vector.tensor_scalar_max(dst, view, 0.0)
            cols = slice(b * GRID, (b + 1) * GRID)

            def quant():
                quantize(
                    h_codes[:, g, cols], h_scales[:, g, cols], hid[:].rearrange("p n t -> p (n t)"), 1024
                )

            pending.append(quant)

        def s2_last(c):
            toks = slice(c * P, (c + 1) * P)
            banks = []
            for n in range(2):
                cols = slice(n * 256, (n + 1) * 256)
                bank = new_bank()
                banks.append(bank)
                for g in range(GROUPS):
                    nc.tensor.matmul_mx(
                        out=bank[:, 0:256],
                        lhsT=h_codes[:, g, toks].bitcast(FP8X4),
                        lhsT_scale=h_scales[:, g, toks],
                        rhs=wo_codes[:, g, cols].bitcast(FP8X4),
                        rhs_scale=wo_scales[:, g, cols],
                        start=(g == 0),
                        stop=(g == GROUPS - 1),
                    )
            for n in range(2):
                half = work.tile([P, 256], F32, name="sorted_x", align_bytes=64)
                if n == 0:
                    nc.scalar.copy(out=half[:], in_=banks[n][:, 0:256])
                else:
                    nc.vector.tensor_copy(out=half[:], in_=banks[n][:, 0:256])
                nc.sync.dma_start(out=out_hbm[toks, n * 256 : (n + 1) * 256], in_=half[:])

        def s2_step(c):
            toks = slice(c * P, (c + 1) * P)
            bank = new_bank()
            for g in range(GROUPS):
                nc.tensor.matmul_mx(
                    out=bank[:],
                    lhsT=h_codes[:, g, toks].bitcast(FP8X4),
                    lhsT_scale=h_scales[:, g, toks],
                    rhs=wo_codes[:, g, :].bitcast(FP8X4),
                    rhs_scale=wo_scales[:, g, :],
                    start=(g == 0),
                    stop=(g == GROUPS - 1),
                )
            flush()
            result = work.tile([P, CH], F32, name="result")
            copy_out(result[:], bank[:], 512)
            nc.sync.dma_start(out=out_hbm[toks, :], in_=result[:])

        warm_bank = new_bank()
        for i in range(12):
            nc.tensor.matmul(warm_bank[:, 0:P], ident_b[:], ident_b[:], start=True, stop=True)
        sort_x(0)
        sobel_step(0)
        w_step(0, 0)
        w_step(0, 1)
        sort_x(1)
        w_step(0, 2)
        sobel_step(1)
        sobel_step(2)
        s1_wide(0, 0)
        sort_w(1, 0)
        sort_w(1, 1)
        sort_w(1, 2)
        s1_wide(0, 1)
        s1_step(0, 4)
        w_step(1, 0)
        w_step(1, 1)
        sort_w(2, 0)
        w_step(1, 2)
        sobel_step(3)
        w_step(2, 0)
        s1_step(0, 5)
        sort_w(2, 1)
        s1_wide(1, 0)
        wo_product(0, 0)
        s1_step(1, 2)
        sort_w(2, 2)
        wo_product(0, 1)
        wo_product(0, 2)
        sort_w(3, 1)
        s1_wide(0, 3)
        sort_w(3, 2)
        wo_product(0, 3)
        s1_step(1, 3)
        wo_product(1, 0)
        w_step(2, 1)
        w_step(3, 0)
        w_step(3, 1)
        w_step(2, 2)
        wo_product(1, 1)
        w_step(3, 2)
        wo_product(1, 2)
        wo_product(1, 3)
        s1_wide(1, 2)
        wo_product(2, 0)
        wo_product(2, 1)
        wo_product(2, 2)
        wo_product(2, 3)
        s1_wide(1, 3)
        wo_product(3, 0)
        sort_wo(0)
        s1_wide(2, 0)
        sort_wo(1)
        s1_wide(2, 1)
        sort_wo(2)
        s1_step(2, 4)
        wo_product(3, 1)
        s1_step(2, 5)
        wo_product(3, 2)
        wo_product(3, 3)
        s1_step(3, 0)
        sort_wo(3)
        s1_wide(3, 1)
        s1_step(3, 1)
        wo_step(0)
        wo_step(1)
        wo_step(2)
        wo_step(3)
        s1_wide(3, 2)
        s1_wide(3, 3)
        s2_step(0)
        s2_step(1)
        s2_step(2)
        s2_step(3)
        s1_wide(2, 3)
        s2_step(4)
        s2_step(5)
        s2_step(6)
        s2_last(7)
